import numpy as np
import ml_dtypes

BF16 = ml_dtypes.bfloat16


def bf(x):
    return np.asarray(x, np.float32).astype(BF16)


def f32(x):
    return np.asarray(x, np.float32)


def f64(x):
    return np.asarray(x).astype(np.float64)


def striped(idx):
    return np.tile(idx.reshape(-1, 16).T, (8, 1))


D, H, S, N = 128, 256, 512, 256
LN_EPS = 1e-5
ERF_LIM = 6.0
ERF_TERMS = 150


def erf(a):
    c = np.clip(a, -ERF_LIM, ERF_LIM)
    term = c.copy()
    tot = c.copy()
    for n in range(1, ERF_TERMS):
        term = term * 2.0 * c * c / (2.0 * n + 1.0)
        tot = tot + term
    r = 2.0 / np.sqrt(np.pi) * np.exp(-c * c) * tot
    return np.where(np.abs(a) > ERF_LIM, np.sign(a), r)


def gelu_erf(v):
    return 0.5 * v * (1.0 + erf(v / np.sqrt(2.0)))


def setup_inputs():
    return {"table": bf(np.random.standard_normal((D, S))), "w1": bf(np.random.standard_normal((D, H)) / np.sqrt(D)), "b1": f32(0.2 * np.random.standard_normal((H, 1))), "gamma": f32(1.0 + 0.1 * np.random.standard_normal((H, 1))), "beta": f32(0.1 * np.random.standard_normal((H, 1))), "w2": bf(np.random.standard_normal((H, D)) / np.sqrt(H)), "b2": f32(0.1 * np.random.standard_normal((D, 1))), "offs": striped(np.random.permutation(S)[:N])}


def reference(table, w1, b1, gamma, beta, w2, b2, offs):
    idx = offs[:16].T.reshape(-1)
    p = f64(w1).T @ f64(table)[:, idx]
    h = gelu_erf(p + f64(b1))
    mu = h.mean(axis=0, keepdims=True)
    var = ((h - mu) ** 2).mean(axis=0, keepdims=True)
    hn = (h - mu) / np.sqrt(var + LN_EPS) * f64(gamma) + f64(beta)
    return f64(w2).T @ hn + f64(b2)

@@ -1,0 +1,84 @@
+import concourse.mybir as mybir
+
+BF16, F32, U16 = mybir.dt.bfloat16, mybir.dt.float32, mybir.dt.uint16
+ACT = mybir.ActivationFunctionType
+ALU = mybir.AluOpType
+
+P = 128
+S = 512
+N = 256
+H = 256
+HB = H // P
+LN_EPS = 1e-5
+
+FLOPS = 2 * P * H * N + 2 * H * P * N
+
+
+def tile_simplepredictor_kernel(tc, table, w1, b1, gamma, beta, w2, b2, offs, out):
+    nc = tc.nc
+    with (
+        tc.tile_pool(name="held", bufs=1) as held,
+        tc.psum_pool(name="psum", bufs=1) as psum,
+    ):
+        offsets = held.tile([P, N // 16], U16, name="offsets")
+        nc.sync.dma_start(offsets[:], offs)
+        table_sb = held.tile([P, S], BF16, name="table_sb")
+        nc.sync.dma_start(table_sb[:], table)
+        w1_sb = held.tile([P, H], BF16, name="w1_sb")
+        nc.scalar.dma_start(w1_sb[:], w1)
+
+        b1_sb = held.tile([P, HB], F32, name="b1_sb")
+        gamma_sb = held.tile([P, HB], F32, name="gamma_sb")
+        beta_sb = held.tile([P, HB], F32, name="beta_sb")
+        b2_sb = held.tile([P, 1], F32, name="b2_sb")
+        w2_sb = held.tile([P, HB, P], BF16, name="w2_sb")
+        with nc.allow_non_contiguous_dma(reason="one float32 to a partition: per-feature vectors"):
+            nc.scalar.dma_start(b1_sb[:], b1.rearrange("(b p) o -> p (b o)", p=P))
+            nc.gpsimd.dma_start(gamma_sb[:], gamma.rearrange("(b p) o -> p (b o)", p=P))
+            nc.gpsimd.dma_start(beta_sb[:], beta.rearrange("(b p) o -> p (b o)", p=P))
+            nc.gpsimd.dma_start(b2_sb[:], b2)
+        nc.gpsimd.dma_start(w2_sb[:], w2.rearrange("(b p) d -> p b d", p=P))
+
+        averager = held.tile([P, P], F32, name="averager")
+        nc.vector.memset(averager[:], 1.0 / H)
+        eps = held.tile([P, 1], F32, name="eps")
+        nc.vector.memset(eps[:], LN_EPS)
+
+        h = held.tile([P, HB, N], F32, name="h")
+        for b in range(HB):
+            pre = psum.tile([P, N], F32, name=f"pre{b}")
+            nc.tensor.matmul(pre[:], w1_sb[:, b * P : (b + 1) * P], table_sb[:].indirect(offsets[:]))
+            nc.scalar.activation(h[:, b, :], pre[:], ACT.Gelu, bias=b1_sb[:, b : b + 1])
+
+        h_sum = held.tile([P, N], F32, name="h_sum")
+        nc.vector.tensor_tensor(h_sum[:], h[:, 0, :], h[:, 1, :], ALU.add)
+        mu = psum.tile([P, N], F32, name="mu")
+        nc.tensor.matmul(mu[:], averager[:], h_sum[:])
+
+        centred = held.tile([P, HB, N], F32, name="centred")
+        squared = held.tile([P, HB, N], F32, name="squared")
+        for b in range(HB):
+            nc.vector.tensor_tensor(centred[:, b, :], h[:, b, :], mu[:], ALU.subtract)
+            nc.vector.tensor_tensor(squared[:, b, :], centred[:, b, :], centred[:, b, :], ALU.mult)
+        sq_sum = held.tile([P, N], F32, name="sq_sum")
+        nc.vector.tensor_tensor(sq_sum[:], squared[:, 0, :], squared[:, 1, :], ALU.add)
+        var = psum.tile([P, N], F32, name="var")
+        nc.tensor.matmul(var[:], averager[:], sq_sum[:])
+
+        rstd = held.tile([P, N], F32, name="rstd")
+        nc.scalar.activation(rstd[:], var[:], ACT.Abs_reciprocal_sqrt, bias=eps[:])
+
+        scaled = held.tile([P, HB, N], F32, name="scaled")
+        hn = held.tile([P, HB, N], BF16, name="hn")
+        acc = psum.tile([P, N], F32, name="acc")
+        for b in range(HB):
+            nc.vector.tensor_tensor(scaled[:, b, :], centred[:, b, :], rstd[:], ALU.mult)
+            nc.scalar.activation(
+                hn[:, b, :], scaled[:, b, :], ACT.Identity,
+                bias=beta_sb[:, b : b + 1], scale=gamma_sb[:, b : b + 1],
+            )
+            nc.tensor.matmul(acc[:], w2_sb[:, b, :], hn[:, b, :], start=(b == 0), stop=(b == HB - 1))
+
+        out_sb = held.tile([P, N], F32, name="out_sb")
+        nc.vector.tensor_scalar(out_sb[:], acc[:], b2_sb[:], None, ALU.add)
+        nc.sync.dma_start(out, out_sb[:])

@@ -34,21 +34,26 @@ def tile_simplepredictor_kernel(tc, table, w1, b1, gamma, beta, w2, b2, offs, ou
         w2_sb = held.tile([P, HB, P], BF16, name="w2_sb")
         with nc.allow_non_contiguous_dma(reason="one float32 to a partition: per-feature vectors"):
             nc.scalar.dma_start(b1_sb[:], b1.rearrange("(b p) o -> p (b o)", p=P))
-            nc.gpsimd.dma_start(gamma_sb[:], gamma.rearrange("(b p) o -> p (b o)", p=P))
-            nc.gpsimd.dma_start(beta_sb[:], beta.rearrange("(b p) o -> p (b o)", p=P))
-            nc.gpsimd.dma_start(b2_sb[:], b2)
-        nc.gpsimd.dma_start(w2_sb[:], w2.rearrange("(b p) d -> p b d", p=P))
+            nc.scalar.dma_start(gamma_sb[:], gamma.rearrange("(b p) o -> p (b o)", p=P))
+            nc.scalar.dma_start(beta_sb[:], beta.rearrange("(b p) o -> p (b o)", p=P))
+            nc.scalar.dma_start(b2_sb[:], b2)
+        nc.sync.dma_start(w2_sb[:], w2.rearrange("(b p) d -> p b d", p=P))
 
         averager = held.tile([P, P], F32, name="averager")
         nc.vector.memset(averager[:], 1.0 / H)
         eps = held.tile([P, 1], F32, name="eps")
         nc.vector.memset(eps[:], LN_EPS)
 
+        table_warmer = held.tile([P, 2], F32, name="table_warmer")
+        nc.scalar.activation(table_warmer[:, 0:1], eps[:], ACT.Gelu)
+
         h = held.tile([P, HB, N], F32, name="h")
         for b in range(HB):
             pre = psum.tile([P, N], F32, name=f"pre{b}")
             nc.tensor.matmul(pre[:], w1_sb[:, b * P : (b + 1) * P], table_sb[:].indirect(offsets[:]))
             nc.scalar.activation(h[:, b, :], pre[:], ACT.Gelu, bias=b1_sb[:, b : b + 1])
+
+        nc.scalar.activation(table_warmer[:, 1:2], h[:, HB - 1, 0:1], ACT.Abs_reciprocal_sqrt)
 
         h_sum = held.tile([P, N], F32, name="h_sum")
         nc.vector.tensor_tensor(h_sum[:], h[:, 0, :], h[:, 1, :], ALU.add)

@@ -1,4 +1,5 @@
 import concourse.mybir as mybir
+from concourse.masks import make_identity
 
 BF16, F32, U16 = mybir.dt.bfloat16, mybir.dt.float32, mybir.dt.uint16
 ACT = mybir.ActivationFunctionType
@@ -9,6 +10,7 @@ S = 512
 N = 256
 H = 256
 HB = H // P
+NB = N // P
 LN_EPS = 1e-5
 
 FLOPS = 2 * P * H * N + 2 * H * P * N
@@ -39,8 +41,8 @@ def tile_simplepredictor_kernel(tc, table, w1, b1, gamma, beta, w2, b2, offs, ou
             nc.scalar.dma_start(b2_sb[:], b2)
         nc.sync.dma_start(w2_sb[:], w2.rearrange("(b p) d -> p b d", p=P))
 
-        averager = held.tile([P, P], F32, name="averager")
-        nc.vector.memset(averager[:], 1.0 / H)
+        identity = held.tile([P, P], F32, name="identity")
+        make_identity(nc, identity[:])
         eps = held.tile([P, 1], F32, name="eps")
         nc.vector.memset(eps[:], LN_EPS)
 
@@ -53,37 +55,49 @@ def tile_simplepredictor_kernel(tc, table, w1, b1, gamma, beta, w2, b2, offs, ou
             nc.tensor.matmul(pre[:], w1_sb[:, b * P : (b + 1) * P], table_sb[:].indirect(offsets[:]))
             nc.scalar.activation(h[:, b, :], pre[:], ACT.Gelu, bias=b1_sb[:, b : b + 1])
 
-        nc.scalar.activation(table_warmer[:, 1:2], h[:, HB - 1, 0:1], ACT.Abs_reciprocal_sqrt)
+        nc.scalar.activation(
+            table_warmer[:, 1:2], h[:, HB - 1, 0:1], ACT.Abs_reciprocal_sqrt, bias=eps[:], scale=0.0
+        )
 
-        h_sum = held.tile([P, N], F32, name="h_sum")
-        nc.vector.tensor_tensor(h_sum[:], h[:, 0, :], h[:, 1, :], ALU.add)
-        mu = psum.tile([P, N], F32, name="mu")
-        nc.tensor.matmul(mu[:], averager[:], h_sum[:])
+        for s in range(NB):
+            samples = slice(s * P, (s + 1) * P)
 
-        centred = held.tile([P, HB, N], F32, name="centred")
-        squared = held.tile([P, HB, N], F32, name="squared")
-        for b in range(HB):
-            nc.vector.tensor_tensor(centred[:, b, :], h[:, b, :], mu[:], ALU.subtract)
-            nc.vector.tensor_tensor(squared[:, b, :], centred[:, b, :], centred[:, b, :], ALU.mult)
-        sq_sum = held.tile([P, N], F32, name="sq_sum")
-        nc.vector.tensor_tensor(sq_sum[:], squared[:, 0, :], squared[:, 1, :], ALU.add)
-        var = psum.tile([P, N], F32, name="var")
-        nc.tensor.matmul(var[:], averager[:], sq_sum[:])
+            flipped = psum.tile([P, H], F32, name=f"flipped{s}")
+            for b in range(HB):
+                nc.tensor.transpose(flipped[:, b * P : (b + 1) * P], h[:, b, samples], identity[:])
 
-        rstd = held.tile([P, N], F32, name="rstd")
-        nc.scalar.activation(rstd[:], var[:], ACT.Abs_reciprocal_sqrt, bias=eps[:])
+            stats = held.tile([P, 6], F32, name=f"stats{s}")
+            nc.vector.bn_stats(stats[:], flipped[:])
+            mean_var = held.tile([P, 2], F32, name=f"mean_var{s}")
+            nc.vector.bn_aggr(mean_var[:], stats[:])
+            rstd = held.tile([P, 1], F32, name=f"rstd{s}")
+            nc.scalar.activation(rstd[:], mean_var[:, 1:2], ACT.Abs_reciprocal_sqrt, bias=eps[:])
 
-        scaled = held.tile([P, HB, N], F32, name="scaled")
-        hn = held.tile([P, HB, N], BF16, name="hn")
-        acc = psum.tile([P, N], F32, name="acc")
-        for b in range(HB):
-            nc.vector.tensor_tensor(scaled[:, b, :], centred[:, b, :], rstd[:], ALU.mult)
-            nc.scalar.activation(
-                hn[:, b, :], scaled[:, b, :], ACT.Identity,
-                bias=beta_sb[:, b : b + 1], scale=gamma_sb[:, b : b + 1],
-            )
-            nc.tensor.matmul(acc[:], w2_sb[:, b, :], hn[:, b, :], start=(b == 0), stop=(b == HB - 1))
+            normed = held.tile([P, H], F32, name=f"normed{s}")
+            nc.vector.tensor_scalar(normed[:], flipped[:], mean_var[:, 0:1], rstd[:], ALU.subtract, ALU.mult)
 
-        out_sb = held.tile([P, N], F32, name="out_sb")
-        nc.vector.tensor_scalar(out_sb[:], acc[:], b2_sb[:], None, ALU.add)
-        nc.sync.dma_start(out, out_sb[:])
+            back = psum.tile([P, HB, P], F32, name=f"back{s}")
+            for b in range(HB):
+                nc.tensor.transpose(back[:, b, :], normed[:, b * P : (b + 1) * P], identity[:])
+
+            hn = held.tile([P, HB, P], BF16, name=f"hn{s}")
+            acc = psum.tile([P, P], F32, name=f"acc{s}")
+            out_sb = held.tile([P, P], F32, name=f"out_sb{s}")
+            for b in range(HB):
+                if s % 2 == 0:
+                    nc.scalar.activation(
+                        hn[:, b, :], back[:, b, :], ACT.Identity,
+                        bias=beta_sb[:, b : b + 1], scale=gamma_sb[:, b : b + 1],
+                    )
+                else:
+                    nc.vector.tensor_scalar(
+                        hn[:, b, :], back[:, b, :], gamma_sb[:, b : b + 1], beta_sb[:, b : b + 1],
+                        ALU.mult, ALU.add,
+                    )
+                nc.tensor.matmul(acc[:], w2_sb[:, b, :], hn[:, b, :], start=(b == 0), stop=(b == HB - 1))
+            if s % 2 == 0:
+                nc.scalar.activation(out_sb[:], acc[:], ACT.Identity, bias=b2_sb[:])
+                nc.sync.dma_start(out[:, samples], out_sb[:])
+            else:
+                nc.vector.tensor_scalar(out_sb[:], acc[:], b2_sb[:], None, ALU.add)
+                nc.scalar.dma_start(out[:, samples], out_sb[:])

@@ -20,14 +20,14 @@ def tile_simplepredictor_kernel(tc, table, w1, b1, gamma, beta, w2, b2, offs, ou
     nc = tc.nc
     with (
         tc.tile_pool(name="held", bufs=1) as held,
-        tc.psum_pool(name="psum", bufs=1) as psum,
+        tc.psum_pool(name="psum", bufs=NB) as psum,
     ):
         offsets = held.tile([P, N // 16], U16, name="offsets")
         nc.sync.dma_start(offsets[:], offs)
         table_sb = held.tile([P, S], BF16, name="table_sb")
-        nc.sync.dma_start(table_sb[:], table)
+        nc.scalar.dma_start(table_sb[:], table)
         w1_sb = held.tile([P, H], BF16, name="w1_sb")
-        nc.scalar.dma_start(w1_sb[:], w1)
+        nc.sync.dma_start(w1_sb[:], w1)
 
         b1_sb = held.tile([P, HB], F32, name="b1_sb")
         gamma_sb = held.tile([P, HB], F32, name="gamma_sb")
@@ -36,9 +36,9 @@ def tile_simplepredictor_kernel(tc, table, w1, b1, gamma, beta, w2, b2, offs, ou
         w2_sb = held.tile([P, HB, P], BF16, name="w2_sb")
         with nc.allow_non_contiguous_dma(reason="one float32 to a partition: per-feature vectors"):
             nc.scalar.dma_start(b1_sb[:], b1.rearrange("(b p) o -> p (b o)", p=P))
-            nc.scalar.dma_start(gamma_sb[:], gamma.rearrange("(b p) o -> p (b o)", p=P))
-            nc.scalar.dma_start(beta_sb[:], beta.rearrange("(b p) o -> p (b o)", p=P))
-            nc.scalar.dma_start(b2_sb[:], b2)
+            nc.sync.dma_start(gamma_sb[:], gamma.rearrange("(b p) o -> p (b o)", p=P))
+            nc.sync.dma_start(beta_sb[:], beta.rearrange("(b p) o -> p (b o)", p=P))
+            nc.sync.dma_start(b2_sb[:], b2)
         nc.sync.dma_start(w2_sb[:], w2.rearrange("(b p) d -> p b d", p=P))
 
         identity = held.tile([P, P], F32, name="identity")
@@ -49,40 +49,39 @@ def tile_simplepredictor_kernel(tc, table, w1, b1, gamma, beta, w2, b2, offs, ou
         table_warmer = held.tile([P, 2], F32, name="table_warmer")
         nc.scalar.activation(table_warmer[:, 0:1], eps[:], ACT.Gelu)
 
-        h = held.tile([P, HB, N], F32, name="h")
-        for b in range(HB):
-            pre = psum.tile([P, N], F32, name=f"pre{b}")
-            nc.tensor.matmul(pre[:], w1_sb[:, b * P : (b + 1) * P], table_sb[:].indirect(offsets[:]))
-            nc.scalar.activation(h[:, b, :], pre[:], ACT.Gelu, bias=b1_sb[:, b : b + 1])
+
+        h = [held.tile([P, HB, P], F32, name=f"h{s}") for s in range(NB)]
+        for s in range(NB):
+            piece = offsets[:, s * (P // 16) : (s + 1) * (P // 16)]
+            for b in range(HB):
+                pre = psum.tile([P, P], F32, name="pre")
+                nc.tensor.matmul(pre[:], w1_sb[:, b * P : (b + 1) * P], table_sb[:].indirect(piece))
+                nc.scalar.activation(h[s][:, b, :], pre[:], ACT.Gelu, bias=b1_sb[:, b : b + 1])
 
         nc.scalar.activation(
-            table_warmer[:, 1:2], h[:, HB - 1, 0:1], ACT.Abs_reciprocal_sqrt, bias=eps[:], scale=0.0
+            table_warmer[:, 1:2], h[NB - 1][:, HB - 1, 0:1], ACT.Abs_reciprocal_sqrt, bias=eps[:], scale=0.0
         )
 
+        normed = [held.tile([P, H], F32, name=f"normed{s}") for s in range(NB)]
         for s in range(NB):
-            samples = slice(s * P, (s + 1) * P)
-
-            flipped = psum.tile([P, H], F32, name=f"flipped{s}")
+            flipped = psum.tile([P, H], F32, name="flipped")
             for b in range(HB):
-                nc.tensor.transpose(flipped[:, b * P : (b + 1) * P], h[:, b, samples], identity[:])
-
+                nc.tensor.transpose(flipped[:, b * P : (b + 1) * P], h[s][:, b, :], identity[:])
             stats = held.tile([P, 6], F32, name=f"stats{s}")
             nc.vector.bn_stats(stats[:], flipped[:])
             mean_var = held.tile([P, 2], F32, name=f"mean_var{s}")
             nc.vector.bn_aggr(mean_var[:], stats[:])
             rstd = held.tile([P, 1], F32, name=f"rstd{s}")
             nc.scalar.activation(rstd[:], mean_var[:, 1:2], ACT.Abs_reciprocal_sqrt, bias=eps[:])
+            nc.vector.tensor_scalar(normed[s][:], flipped[:], mean_var[:, 0:1], rstd[:], ALU.subtract, ALU.mult)
 
-            normed = held.tile([P, H], F32, name=f"normed{s}")
-            nc.vector.tensor_scalar(normed[:], flipped[:], mean_var[:, 0:1], rstd[:], ALU.subtract, ALU.mult)
-
-            back = psum.tile([P, HB, P], F32, name=f"back{s}")
-            for b in range(HB):
-                nc.tensor.transpose(back[:, b, :], normed[:, b * P : (b + 1) * P], identity[:])
-
+        for s in range(NB):
+            back = psum.tile([P, HB, P], F32, name="back")
             hn = held.tile([P, HB, P], BF16, name=f"hn{s}")
-            acc = psum.tile([P, P], F32, name=f"acc{s}")
+            acc = psum.tile([P, P], F32, name="acc")
             out_sb = held.tile([P, P], F32, name=f"out_sb{s}")
+            for b in range(HB):
+                nc.tensor.transpose(back[:, b, :], normed[s][:, b * P : (b + 1) * P], identity[:])
             for b in range(HB):
                 if s % 2 == 0:
                     nc.scalar.activation(
@@ -97,7 +96,7 @@ def tile_simplepredictor_kernel(tc, table, w1, b1, gamma, beta, w2, b2, offs, ou
                 nc.tensor.matmul(acc[:], w2_sb[:, b, :], hn[:, b, :], start=(b == 0), stop=(b == HB - 1))
             if s % 2 == 0:
                 nc.scalar.activation(out_sb[:], acc[:], ACT.Identity, bias=b2_sb[:])
-                nc.sync.dma_start(out[:, samples], out_sb[:])
+                nc.sync.dma_start(out[:, s * P : (s + 1) * P], out_sb[:])
             else:
                 nc.vector.tensor_scalar(out_sb[:], acc[:], b2_sb[:], None, ALU.add)
-                nc.scalar.dma_start(out[:, samples], out_sb[:])
+                nc.scalar.dma_start(out[:, s * P : (s + 1) * P], out_sb[:])

@@ -20,14 +20,14 @@ def tile_simplepredictor_kernel(tc, table, w1, b1, gamma, beta, w2, b2, offs, ou
     nc = tc.nc
     with (
         tc.tile_pool(name="held", bufs=1) as held,
-        tc.psum_pool(name="psum", bufs=NB) as psum,
+        tc.psum_pool(name="psum", bufs=1) as psum,
     ):
         offsets = held.tile([P, N // 16], U16, name="offsets")
         nc.sync.dma_start(offsets[:], offs)
         table_sb = held.tile([P, S], BF16, name="table_sb")
-        nc.scalar.dma_start(table_sb[:], table)
+        nc.sync.dma_start(table_sb[:], table)
         w1_sb = held.tile([P, H], BF16, name="w1_sb")
-        nc.sync.dma_start(w1_sb[:], w1)
+        nc.scalar.dma_start(w1_sb[:], w1)
 
         b1_sb = held.tile([P, HB], F32, name="b1_sb")
         gamma_sb = held.tile([P, HB], F32, name="gamma_sb")
@@ -36,9 +36,9 @@ def tile_simplepredictor_kernel(tc, table, w1, b1, gamma, beta, w2, b2, offs, ou
         w2_sb = held.tile([P, HB, P], BF16, name="w2_sb")
         with nc.allow_non_contiguous_dma(reason="one float32 to a partition: per-feature vectors"):
             nc.scalar.dma_start(b1_sb[:], b1.rearrange("(b p) o -> p (b o)", p=P))
-            nc.sync.dma_start(gamma_sb[:], gamma.rearrange("(b p) o -> p (b o)", p=P))
-            nc.sync.dma_start(beta_sb[:], beta.rearrange("(b p) o -> p (b o)", p=P))
-            nc.sync.dma_start(b2_sb[:], b2)
+            nc.scalar.dma_start(gamma_sb[:], gamma.rearrange("(b p) o -> p (b o)", p=P))
+            nc.scalar.dma_start(beta_sb[:], beta.rearrange("(b p) o -> p (b o)", p=P))
+            nc.scalar.dma_start(b2_sb[:], b2)
         nc.sync.dma_start(w2_sb[:], w2.rearrange("(b p) d -> p b d", p=P))
 
         identity = held.tile([P, P], F32, name="identity")
@@ -50,35 +50,38 @@ def tile_simplepredictor_kernel(tc, table, w1, b1, gamma, beta, w2, b2, offs, ou
         nc.scalar.activation(table_warmer[:, 0:1], eps[:], ACT.Gelu)
 
 
-        h = [held.tile([P, HB, P], F32, name=f"h{s}") for s in range(NB)]
-        for s in range(NB):
-            piece = offsets[:, s * (P // 16) : (s + 1) * (P // 16)]
-            for b in range(HB):
-                pre = psum.tile([P, P], F32, name="pre")
-                nc.tensor.matmul(pre[:], w1_sb[:, b * P : (b + 1) * P], table_sb[:].indirect(piece))
-                nc.scalar.activation(h[s][:, b, :], pre[:], ACT.Gelu, bias=b1_sb[:, b : b + 1])
+        h = held.tile([P, HB, N], F32, name="h")
+        for b in range(HB):
+            pre = psum.tile([P, N], F32, name=f"pre{b}")
+            nc.tensor.matmul(pre[:], w1_sb[:, b * P : (b + 1) * P], table_sb[:].indirect(offsets[:]))
+            nc.scalar.activation(h[:, b, :], pre[:], ACT.Gelu, bias=b1_sb[:, b : b + 1])
 
         nc.scalar.activation(
-            table_warmer[:, 1:2], h[NB - 1][:, HB - 1, 0:1], ACT.Abs_reciprocal_sqrt, bias=eps[:], scale=0.0
+            table_warmer[:, 1:2], h[:, HB - 1, 0:1], ACT.Abs_reciprocal_sqrt, bias=eps[:], scale=0.0
         )
 
+
+        flipped = [psum.tile([P, H], F32, name=f"flipped{s}") for s in range(NB)]
         normed = [held.tile([P, H], F32, name=f"normed{s}") for s in range(NB)]
+        for b in range(HB):
+            for s in range(NB):
+                nc.tensor.transpose(flipped[s][:, b * P : (b + 1) * P], h[:, b, s * P : (s + 1) * P], identity[:])
+        mean_var = held.tile([P, NB, 2], F32, name="mean_var")
         for s in range(NB):
-            flipped = psum.tile([P, H], F32, name="flipped")
-            for b in range(HB):
-                nc.tensor.transpose(flipped[:, b * P : (b + 1) * P], h[s][:, b, :], identity[:])
             stats = held.tile([P, 6], F32, name=f"stats{s}")
-            nc.vector.bn_stats(stats[:], flipped[:])
-            mean_var = held.tile([P, 2], F32, name=f"mean_var{s}")
-            nc.vector.bn_aggr(mean_var[:], stats[:])
-            rstd = held.tile([P, 1], F32, name=f"rstd{s}")
-            nc.scalar.activation(rstd[:], mean_var[:, 1:2], ACT.Abs_reciprocal_sqrt, bias=eps[:])
-            nc.vector.tensor_scalar(normed[s][:], flipped[:], mean_var[:, 0:1], rstd[:], ALU.subtract, ALU.mult)
+            nc.vector.bn_stats(stats[:], flipped[s][:])
+            nc.vector.bn_aggr(mean_var[:, s, :], stats[:])
+        rstd = held.tile([P, NB], F32, name="rstd")
+        nc.scalar.activation(rstd[:], mean_var[:, :, 1], ACT.Abs_reciprocal_sqrt, bias=eps[:])
+        for s in range(NB):
+            nc.vector.tensor_scalar(
+                normed[s][:], flipped[s][:], mean_var[:, s, 0:1], rstd[:, s : s + 1], ALU.subtract, ALU.mult
+            )
 
         for s in range(NB):
-            back = psum.tile([P, HB, P], F32, name="back")
+            back = psum.tile([P, HB, P], F32, name=f"back{s}")
             hn = held.tile([P, HB, P], BF16, name=f"hn{s}")
-            acc = psum.tile([P, P], F32, name="acc")
+            acc = psum.tile([P, P], F32, name=f"acc{s}")
             out_sb = held.tile([P, P], F32, name=f"out_sb{s}")
             for b in range(HB):
                 nc.tensor.transpose(back[:, b, :], normed[s][:, b * P : (b + 1) * P], identity[:])

@@ -12,6 +12,7 @@ H = 256
 HB = H // P
 NB = N // P
 LN_EPS = 1e-5
+WARM_UP_MATMULS = 5
 
 FLOPS = 2 * P * H * N + 2 * H * P * N
 
@@ -41,6 +42,13 @@ def tile_simplepredictor_kernel(tc, table, w1, b1, gamma, beta, w2, b2, offs, ou
             nc.scalar.dma_start(b2_sb[:], b2)
         nc.sync.dma_start(w2_sb[:], w2.rearrange("(b p) d -> p b d", p=P))
 
+
+        zeros = held.tile([P, N], BF16, name="zeros")
+        nc.vector.memset(zeros[:], 0.0)
+        unused = psum.tile([P, N], F32, name="unused", tag="acc1")
+        for i in range(WARM_UP_MATMULS):
+            nc.tensor.matmul(unused[:], zeros[:, 0:P], zeros[:])
+
         identity = held.tile([P, P], F32, name="identity")
         make_identity(nc, identity[:])
         eps = held.tile([P, 1], F32, name="eps")
@@ -63,20 +71,17 @@ def tile_simplepredictor_kernel(tc, table, w1, b1, gamma, beta, w2, b2, offs, ou
 
         flipped = [psum.tile([P, H], F32, name=f"flipped{s}") for s in range(NB)]
         normed = [held.tile([P, H], F32, name=f"normed{s}") for s in range(NB)]
-        for b in range(HB):
-            for s in range(NB):
+        for s in range(NB):
+            for b in range(HB):
                 nc.tensor.transpose(flipped[s][:, b * P : (b + 1) * P], h[:, b, s * P : (s + 1) * P], identity[:])
-        mean_var = held.tile([P, NB, 2], F32, name="mean_var")
         for s in range(NB):
             stats = held.tile([P, 6], F32, name=f"stats{s}")
             nc.vector.bn_stats(stats[:], flipped[s][:])
-            nc.vector.bn_aggr(mean_var[:, s, :], stats[:])
-        rstd = held.tile([P, NB], F32, name="rstd")
-        nc.scalar.activation(rstd[:], mean_var[:, :, 1], ACT.Abs_reciprocal_sqrt, bias=eps[:])
-        for s in range(NB):
-            nc.vector.tensor_scalar(
-                normed[s][:], flipped[s][:], mean_var[:, s, 0:1], rstd[:, s : s + 1], ALU.subtract, ALU.mult
-            )
+            mean_var = held.tile([P, 2], F32, name=f"mean_var{s}")
+            nc.vector.bn_aggr(mean_var[:], stats[:])
+            rstd = held.tile([P, 1], F32, name=f"rstd{s}")
+            nc.scalar.activation(rstd[:], mean_var[:, 1:2], ACT.Abs_reciprocal_sqrt, bias=eps[:])
+            nc.vector.tensor_scalar(normed[s][:], flipped[s][:], mean_var[:, 0:1], rstd[:], ALU.subtract, ALU.mult)
 
         for s in range(NB):
             back = psum.tile([P, HB, P], F32, name=f"back{s}")

@@ -23,10 +23,10 @@ def tile_simplepredictor_kernel(tc, table, w1, b1, gamma, beta, w2, b2, offs, ou
         tc.tile_pool(name="held", bufs=1) as held,
         tc.psum_pool(name="psum", bufs=1) as psum,
     ):
-        offsets = held.tile([P, N // 16], U16, name="offsets")
-        nc.sync.dma_start(offsets[:], offs)
         table_sb = held.tile([P, S], BF16, name="table_sb")
         nc.sync.dma_start(table_sb[:], table)
+        offsets = held.tile([P, N // 16], U16, name="offsets")
+        nc.sync.dma_start(offsets[:], offs)
         w1_sb = held.tile([P, H], BF16, name="w1_sb")
         nc.scalar.dma_start(w1_sb[:], w1)
 
@@ -84,23 +84,20 @@ def tile_simplepredictor_kernel(tc, table, w1, b1, gamma, beta, w2, b2, offs, ou
             nc.vector.tensor_scalar(normed[s][:], flipped[s][:], mean_var[:, 0:1], rstd[:], ALU.subtract, ALU.mult)
 
         for s in range(NB):
-            back = psum.tile([P, HB, P], F32, name=f"back{s}")
+            back = [
+                psum.tile([P, P], F32, name=f"back{s}{b}", tag=(f"pre{b}" if s == 0 else f"back{b}"))
+                for b in range(HB)
+            ]
             hn = held.tile([P, HB, P], BF16, name=f"hn{s}")
             acc = psum.tile([P, P], F32, name=f"acc{s}")
             out_sb = held.tile([P, P], F32, name=f"out_sb{s}")
             for b in range(HB):
-                nc.tensor.transpose(back[:, b, :], normed[s][:, b * P : (b + 1) * P], identity[:])
+                nc.tensor.transpose(back[b][:], normed[s][:, b * P : (b + 1) * P], identity[:])
+            nc.scalar.activation(
+                hn[:, 0, :], back[0][:], ACT.Identity, bias=beta_sb[:, 0:1], scale=gamma_sb[:, 0:1]
+            )
+            nc.vector.tensor_scalar(hn[:, 1, :], back[1][:], gamma_sb[:, 1:2], beta_sb[:, 1:2], ALU.mult, ALU.add)
             for b in range(HB):
-                if s % 2 == 0:
-                    nc.scalar.activation(
-                        hn[:, b, :], back[:, b, :], ACT.Identity,
-                        bias=beta_sb[:, b : b + 1], scale=gamma_sb[:, b : b + 1],
-                    )
-                else:
-                    nc.vector.tensor_scalar(
-                        hn[:, b, :], back[:, b, :], gamma_sb[:, b : b + 1], beta_sb[:, b : b + 1],
-                        ALU.mult, ALU.add,
-                    )
                 nc.tensor.matmul(acc[:], w2_sb[:, b, :], hn[:, b, :], start=(b == 0), stop=(b == HB - 1))
             if s % 2 == 0:
                 nc.scalar.activation(out_sb[:], acc[:], ACT.Identity, bias=b2_sb[:])

@@ -74,6 +74,10 @@ def tile_simplepredictor_kernel(tc, table, w1, b1, gamma, beta, w2, b2, offs, ou
         for s in range(NB):
             for b in range(HB):
                 nc.tensor.transpose(flipped[s][:, b * P : (b + 1) * P], h[:, b, s * P : (s + 1) * P], identity[:])
+
+        unused_again = psum.tile([P, N], F32, name="unused_again", tag="acc1")
+        nc.tensor.matmul(unused_again[:], identity[:], h[:, HB - 1, :])
+
         for s in range(NB):
             stats = held.tile([P, 6], F32, name=f"stats{s}")
             nc.vector.bn_stats(stats[:], flipped[s][:])

@@ -85,7 +85,11 @@ def tile_simplepredictor_kernel(tc, table, w1, b1, gamma, beta, w2, b2, offs, ou
             nc.vector.bn_aggr(mean_var[:], stats[:])
             rstd = held.tile([P, 1], F32, name=f"rstd{s}")
             nc.scalar.activation(rstd[:], mean_var[:, 1:2], ACT.Abs_reciprocal_sqrt, bias=eps[:])
-            nc.vector.tensor_scalar(normed[s][:], flipped[s][:], mean_var[:, 0:1], rstd[:], ALU.subtract, ALU.mult)
+            for b in range(HB):
+                nc.vector.tensor_scalar(
+                    normed[s][:, b * P : (b + 1) * P], flipped[s][:, b * P : (b + 1) * P],
+                    mean_var[:, 0:1], rstd[:], ALU.subtract, ALU.mult,
+                )
 
         for s in range(NB):
             back = [

@@ -45,7 +45,7 @@ def tile_simplepredictor_kernel(tc, table, w1, b1, gamma, beta, w2, b2, offs, ou
 
         zeros = held.tile([P, N], BF16, name="zeros")
         nc.vector.memset(zeros[:], 0.0)
-        unused = psum.tile([P, N], F32, name="unused", tag="acc1")
+        unused = psum.tile([P, N], F32, name="unused", tag="unused")
         for i in range(WARM_UP_MATMULS):
             nc.tensor.matmul(unused[:], zeros[:, 0:P], zeros[:])
 
@@ -69,35 +69,33 @@ def tile_simplepredictor_kernel(tc, table, w1, b1, gamma, beta, w2, b2, offs, ou
         )
 
 
-        flipped = [psum.tile([P, H], F32, name=f"flipped{s}") for s in range(NB)]
+        flipped = [[psum.tile([P, P], F32, name=f"flipped{s}{b}") for b in range(HB)] for s in range(NB)]
         normed = [held.tile([P, H], F32, name=f"normed{s}") for s in range(NB)]
-        for s in range(NB):
-            for b in range(HB):
-                nc.tensor.transpose(flipped[s][:, b * P : (b + 1) * P], h[:, b, s * P : (s + 1) * P], identity[:])
+        stats = [held.tile([P, HB * 6], F32, name=f"stats{s}") for s in range(NB)]
+        for b in range(HB):
+            for s in range(NB):
+                nc.tensor.transpose(flipped[s][b][:], h[:, b, s * P : (s + 1) * P], identity[:])
+                nc.vector.bn_stats(stats[s][:, b * 6 : (b + 1) * 6], flipped[s][b][:])
 
-        unused_again = psum.tile([P, N], F32, name="unused_again", tag="acc1")
+        unused_again = psum.tile([P, N], F32, name="unused_again", tag="unused")
         nc.tensor.matmul(unused_again[:], identity[:], h[:, HB - 1, :])
 
         for s in range(NB):
-            stats = held.tile([P, 6], F32, name=f"stats{s}")
-            nc.vector.bn_stats(stats[:], flipped[s][:])
             mean_var = held.tile([P, 2], F32, name=f"mean_var{s}")
-            nc.vector.bn_aggr(mean_var[:], stats[:])
+            nc.vector.bn_aggr(mean_var[:], stats[s][:])
             rstd = held.tile([P, 1], F32, name=f"rstd{s}")
             nc.scalar.activation(rstd[:], mean_var[:, 1:2], ACT.Abs_reciprocal_sqrt, bias=eps[:])
             for b in range(HB):
                 nc.vector.tensor_scalar(
-                    normed[s][:, b * P : (b + 1) * P], flipped[s][:, b * P : (b + 1) * P],
+                    normed[s][:, b * P : (b + 1) * P], flipped[s][b][:],
                     mean_var[:, 0:1], rstd[:], ALU.subtract, ALU.mult,
                 )
 
+        back_tag = [["pre0", "pre1"], ["flipped01", "back11"]]
         for s in range(NB):
-            back = [
-                psum.tile([P, P], F32, name=f"back{s}{b}", tag=(f"pre{b}" if s == 0 else f"back{b}"))
-                for b in range(HB)
-            ]
+            back = [psum.tile([P, P], F32, name=f"back{s}{b}", tag=back_tag[s][b]) for b in range(HB)]
             hn = held.tile([P, HB, P], BF16, name=f"hn{s}")
-            acc = psum.tile([P, P], F32, name=f"acc{s}")
+            acc = psum.tile([P, P], F32, name=f"acc{s}", tag=f"flipped{s}0")
             out_sb = held.tile([P, P], F32, name=f"out_sb{s}")
             for b in range(HB):
                 nc.tensor.transpose(back[b][:], normed[s][:, b * P : (b + 1) * P], identity[:])

@@ -80,15 +80,21 @@ def tile_simplepredictor_kernel(tc, table, w1, b1, gamma, beta, w2, b2, offs, ou
         unused_again = psum.tile([P, N], F32, name="unused_again", tag="unused")
         nc.tensor.matmul(unused_again[:], identity[:], h[:, HB - 1, :])
 
+        mean_var = [held.tile([P, 2], F32, name=f"mean_var{s}") for s in range(NB)]
+        rstd = [held.tile([P, 1], F32, name=f"rstd{s}") for s in range(NB)]
         for s in range(NB):
-            mean_var = held.tile([P, 2], F32, name=f"mean_var{s}")
-            nc.vector.bn_aggr(mean_var[:], stats[s][:])
-            rstd = held.tile([P, 1], F32, name=f"rstd{s}")
-            nc.scalar.activation(rstd[:], mean_var[:, 1:2], ACT.Abs_reciprocal_sqrt, bias=eps[:])
+            nc.vector.bn_aggr(mean_var[s][:], stats[s][:])
+            nc.scalar.activation(rstd[s][:], mean_var[s][:, 1:2], ACT.Abs_reciprocal_sqrt, bias=eps[:])
+        centred = [held.tile([P, H], F32, name=f"centred{s}") for s in range(NB)]
+        for s in range(NB):
             for b in range(HB):
                 nc.vector.tensor_scalar(
-                    normed[s][:, b * P : (b + 1) * P], flipped[s][b][:],
-                    mean_var[:, 0:1], rstd[:], ALU.subtract, ALU.mult,
+                    centred[s][:, b * P : (b + 1) * P], flipped[s][b][:], mean_var[s][:, 0:1], None, ALU.subtract
+                )
+        for s in range(NB):
+            for b in range(HB):
+                nc.vector.tensor_scalar(
+                    normed[s][:, b * P : (b + 1) * P], centred[s][:, b * P : (b + 1) * P], rstd[s][:], None, ALU.mult
                 )
 
         back_tag = [["pre0", "pre1"], ["flipped01", "back11"]]

@@ -77,8 +77,9 @@ def tile_simplepredictor_kernel(tc, table, w1, b1, gamma, beta, w2, b2, offs, ou
                 nc.tensor.transpose(flipped[s][b][:], h[:, b, s * P : (s + 1) * P], identity[:])
                 nc.vector.bn_stats(stats[s][:, b * 6 : (b + 1) * 6], flipped[s][b][:])
 
-        unused_again = psum.tile([P, N], F32, name="unused_again", tag="unused")
-        nc.tensor.matmul(unused_again[:], identity[:], h[:, HB - 1, :])
+        unused_again = psum.tile([P, N + P], F32, name="unused_again", tag="unused")
+        nc.tensor.matmul(unused_again[:, 0:N], identity[:], h[:, HB - 1, :])
+        nc.tensor.matmul(unused_again[:, N : N + P], identity[:], h[:, HB - 1, 0:P])
 
         mean_var = [held.tile([P, 2], F32, name=f"mean_var{s}") for s in range(NB)]
         rstd = [held.tile([P, 1], F32, name=f"rstd{s}") for s in range(NB)]

import concourse.mybir as mybir
from concourse.masks import make_identity

BF16, F32, U16 = mybir.dt.bfloat16, mybir.dt.float32, mybir.dt.uint16
ACT = mybir.ActivationFunctionType
ALU = mybir.AluOpType

P = 128
S = 512
N = 256
H = 256
HB = H // P
NB = N // P
LN_EPS = 1e-5
WARM_UP_MATMULS = 5

FLOPS = 2 * P * H * N + 2 * H * P * N


def tile_simplepredictor_kernel(tc, table, w1, b1, gamma, beta, w2, b2, offs, out):
    nc = tc.nc
    with (
        tc.tile_pool(name="held", bufs=1) as held,
        tc.psum_pool(name="psum", bufs=1) as psum,
    ):
        table_sb = held.tile([P, S], BF16, name="table_sb")
        nc.sync.dma_start(table_sb[:], table)
        offsets = held.tile([P, N // 16], U16, name="offsets")
        nc.sync.dma_start(offsets[:], offs)
        w1_sb = held.tile([P, H], BF16, name="w1_sb")
        nc.scalar.dma_start(w1_sb[:], w1)

        b1_sb = held.tile([P, HB], F32, name="b1_sb")
        gamma_sb = held.tile([P, HB], F32, name="gamma_sb")
        beta_sb = held.tile([P, HB], F32, name="beta_sb")
        b2_sb = held.tile([P, 1], F32, name="b2_sb")
        w2_sb = held.tile([P, HB, P], BF16, name="w2_sb")
        with nc.allow_non_contiguous_dma(reason="one float32 to a partition: per-feature vectors"):
            nc.scalar.dma_start(b1_sb[:], b1.rearrange("(b p) o -> p (b o)", p=P))
            nc.scalar.dma_start(gamma_sb[:], gamma.rearrange("(b p) o -> p (b o)", p=P))
            nc.scalar.dma_start(beta_sb[:], beta.rearrange("(b p) o -> p (b o)", p=P))
            nc.scalar.dma_start(b2_sb[:], b2)
        nc.sync.dma_start(w2_sb[:], w2.rearrange("(b p) d -> p b d", p=P))


        zeros = held.tile([P, N], BF16, name="zeros")
        nc.vector.memset(zeros[:], 0.0)
        unused = psum.tile([P, N], F32, name="unused", tag="unused")
        for i in range(WARM_UP_MATMULS):
            nc.tensor.matmul(unused[:], zeros[:, 0:P], zeros[:])

        identity = held.tile([P, P], F32, name="identity")
        make_identity(nc, identity[:])
        eps = held.tile([P, 1], F32, name="eps")
        nc.vector.memset(eps[:], LN_EPS)

        table_warmer = held.tile([P, 2], F32, name="table_warmer")
        nc.scalar.activation(table_warmer[:, 0:1], eps[:], ACT.Gelu)


        h = held.tile([P, HB, N], F32, name="h")
        for b in range(HB):
            pre = psum.tile([P, N], F32, name=f"pre{b}")
            nc.tensor.matmul(pre[:], w1_sb[:, b * P : (b + 1) * P], table_sb[:].indirect(offsets[:]))
            nc.scalar.activation(h[:, b, :], pre[:], ACT.Gelu, bias=b1_sb[:, b : b + 1])

        nc.scalar.activation(
            table_warmer[:, 1:2], h[:, HB - 1, 0:1], ACT.Abs_reciprocal_sqrt, bias=eps[:], scale=0.0
        )


        flipped = [[psum.tile([P, P], F32, name=f"flipped{s}{b}") for b in range(HB)] for s in range(NB)]
        normed = [held.tile([P, H], F32, name=f"normed{s}") for s in range(NB)]
        stats = [held.tile([P, HB * 6], F32, name=f"stats{s}") for s in range(NB)]
        for b in range(HB):
            for s in range(NB):
                nc.tensor.transpose(flipped[s][b][:], h[:, b, s * P : (s + 1) * P], identity[:])
                nc.vector.bn_stats(stats[s][:, b * 6 : (b + 1) * 6], flipped[s][b][:])

        unused_again = psum.tile([P, N + P], F32, name="unused_again", tag="unused")
        nc.tensor.matmul(unused_again[:, 0:N], identity[:], h[:, HB - 1, :])
        nc.tensor.matmul(unused_again[:, N : N + P], identity[:], h[:, HB - 1, 0:P])

        mean_var = [held.tile([P, 2], F32, name=f"mean_var{s}") for s in range(NB)]
        rstd = [held.tile([P, 1], F32, name=f"rstd{s}") for s in range(NB)]
        for s in range(NB):
            nc.vector.bn_aggr(mean_var[s][:], stats[s][:])
            nc.scalar.activation(rstd[s][:], mean_var[s][:, 1:2], ACT.Abs_reciprocal_sqrt, bias=eps[:])
        centred = [held.tile([P, H], F32, name=f"centred{s}") for s in range(NB)]
        for s in range(NB):
            for b in range(HB):
                nc.vector.tensor_scalar(
                    centred[s][:, b * P : (b + 1) * P], flipped[s][b][:], mean_var[s][:, 0:1], None, ALU.subtract
                )
        for s in range(NB):
            for b in range(HB):
                nc.vector.tensor_scalar(
                    normed[s][:, b * P : (b + 1) * P], centred[s][:, b * P : (b + 1) * P], rstd[s][:], None, ALU.mult
                )

        back_tag = [["pre0", "pre1"], ["flipped01", "back11"]]
        for s in range(NB):
            back = [psum.tile([P, P], F32, name=f"back{s}{b}", tag=back_tag[s][b]) for b in range(HB)]
            hn = held.tile([P, HB, P], BF16, name=f"hn{s}")
            acc = psum.tile([P, P], F32, name=f"acc{s}", tag=f"flipped{s}0")
            out_sb = held.tile([P, P], F32, name=f"out_sb{s}")
            for b in range(HB):
                nc.tensor.transpose(back[b][:], normed[s][:, b * P : (b + 1) * P], identity[:])
            nc.scalar.activation(
                hn[:, 0, :], back[0][:], ACT.Identity, bias=beta_sb[:, 0:1], scale=gamma_sb[:, 0:1]
            )
            nc.vector.tensor_scalar(hn[:, 1, :], back[1][:], gamma_sb[:, 1:2], beta_sb[:, 1:2], ALU.mult, ALU.add)
            for b in range(HB):
                nc.tensor.matmul(acc[:], w2_sb[:, b, :], hn[:, b, :], start=(b == 0), stop=(b == HB - 1))
            if s % 2 == 0:
                nc.scalar.activation(out_sb[:], acc[:], ACT.Identity, bias=b2_sb[:])
                nc.sync.dma_start(out[:, s * P : (s + 1) * P], out_sb[:])
            else:
                nc.vector.tensor_scalar(out_sb[:], acc[:], b2_sb[:], None, ALU.add)
                nc.scalar.dma_start(out[:, s * P : (s + 1) * P], out_sb[:])
